import numpy as np
import ml_dtypes


def mxq(x, axis, fmt="e4m3"):
    dtype, down = {"e4m3": (ml_dtypes.float8_e4m3fn, 7), "e5m2": (ml_dtypes.float8_e5m2, 14)}[fmt]
    v = np.moveaxis(np.asarray(x, np.float32).astype(ml_dtypes.bfloat16).astype(np.float64), axis, -1)
    blocks = v.reshape(v.shape[:-1] + (-1, 32))
    amax = np.abs(blocks).max(-1, keepdims=True)
    byte = np.maximum(np.where(amax > 0, np.frexp(amax)[1] - 1 + 127, 0) - down, 1)
    scale = np.exp2(byte - 127.0)
    codes = (blocks / scale).astype(np.float32).astype(dtype).astype(np.float64)
    return np.moveaxis((codes * scale).reshape(v.shape), -1, axis)


WIDE = False


def mx_kscale(k):
    if not WIDE:
        return np.ones(k)
    levels = np.array([10, -10, 5, -5, 0])
    a = np.random.permutation(np.resize(levels, k // 512 * 4)).reshape(k // 512, 4)
    idx = np.arange(k)
    return np.exp2(a[idx // 512, idx % 128 // 32])


BF16 = ml_dtypes.bfloat16


def bf(x):
    return np.asarray(x, np.float32).astype(BF16)


def f64(x):
    return np.asarray(x).astype(np.float64)


B, E, LATENT, COND, HIDDEN, OUT, GH = 1024, 8, 128, 384, 384, 256, 128
INPUT = LATENT + COND
EPS = 1e-5


def elu(v):
    return np.where(v > 0.0, v, np.exp(np.minimum(v, 0.0)) - 1.0)


def layernorm(v):
    mu = v.mean(-1, keepdims=True)
    var = np.square(v - mu).mean(-1, keepdims=True)
    return (v - mu) / np.sqrt(var + EPS)


def softmax(v):
    e = np.exp(v - v.max(-1, keepdims=True))
    return e / e.sum(-1, keepdims=True)


def setup_inputs():
    rn = np.random.standard_normal
    swap = np.arange(INPUT) ^ 1
    s = f64(mx_kscale(INPUT))
    s = np.minimum(s, s[swap])
    g = np.exp2(np.round(np.log2(np.sqrt(np.mean(s * s)))))
    u = rn((B, INPUT))
    pair = f64(bf((u - u[:, swap]) * np.sqrt(0.5)))
    gen = np.concatenate([0.5 * rn((B, LATENT)), 0.4 + rn((B, COND))], axis=1)
    x = pair * s + np.min(s) ** 3 * gen
    return {"z": bf(x[:, :LATENT]),
            "c": bf(x[:, LATENT:]),
            "gate_logits": bf(1.5 * rn((B, E))),
            "w0": bf(rn((E, INPUT, HIDDEN)) * 1.5 / np.sqrt(INPUT) / s[None, :, None] * g),
            "b0": bf(rn((E, HIDDEN)) * 0.5)}


def reference(z, c, gate_logits, w0, b0):
    coeff = softmax(f64(gate_logits))
    inp = layernorm(np.concatenate([f64(z), f64(c)], axis=-1))
    y = mxq(inp, 1, "e4m3") @ mxq(f64(w0), 1, "e4m3")
    mixed = (coeff.T[:, :, None] * y).sum(0)
    mixed_bias = (coeff[:, :, None] * f64(b0)[None]).sum(1)
    return elu(mixed + mixed_bias)

@@ -1,0 +1,203 @@
+from contextlib import ExitStack
+
+import concourse.mybir as mybir
+from concourse.masks import make_identity
+
+F32 = mybir.dt.float32
+BF16 = mybir.dt.bfloat16
+U32 = mybir.dt.uint32
+U8 = mybir.dt.uint8
+FP8X4 = mybir.dt.float8_e4m3fn_x4
+ALU = mybir.AluOpType
+ACT = mybir.ActivationFunctionType
+AXIS = mybir.AxisListType
+
+P = 128
+PACK = 4
+ROWS, EXPERTS, LATENT, COND, HIDDEN = 1024, 8, 128, 384, 384
+FEATURES = LATENT + COND
+ROW_TILES = ROWS // P
+HALF = ROW_TILES // 2
+PAIR = 2
+EPS = 1e-5
+WIDE, NARROW = 256, 128
+RUN = 4
+
+SCALAR_TEAM_TILES = 3
+
+FLOPS = 2 * ROWS * FEATURES * HIDDEN * EXPERTS
+
+
+def in_scalar_team(i):
+    return i % 2 == 1 and i // 2 < SCALAR_TEAM_TILES
+
+
+def tile_gatingmixeddecoder_pa_kernel(tc, z, c, gate_logits, w0, b0, out):
+    nc = tc.nc
+    z_rows = z.rearrange("(p i) f -> p i f", i=ROW_TILES)
+    c_rows = c.rearrange("(p i) f -> p i f", i=ROW_TILES)
+    logit_rows = gate_logits.rearrange("(p i) e -> p i e", i=ROW_TILES)
+    out_rows = out.rearrange("(p i) h -> p i h", i=ROW_TILES)
+
+    with ExitStack() as ctx:
+        keep = ctx.enter_context(tc.tile_pool(name="keep", bufs=1))
+        work = ctx.enter_context(tc.tile_pool(name="work", bufs=3))
+        psum_t = ctx.enter_context(tc.psum_pool(name="psum_t", bufs=2))
+        psum_vector = ctx.enter_context(tc.psum_pool(name="psum_vector", bufs=3))
+        psum_scalar = ctx.enter_context(tc.psum_pool(name="psum_scalar", bufs=3))
+
+        def product_pool(i):
+            return psum_scalar if in_scalar_team(i) else psum_vector
+
+        ident = keep.tile([P, P], BF16)
+        make_identity(nc, ident[:])
+        eps_col = keep.tile([P, 1], F32)
+        nc.vector.memset(eps_col[:], EPS)
+        bias_rows = keep.tile([P, HIDDEN], BF16)
+        nc.vector.memset(bias_rows[:], 0.0)
+        coeff_cols = keep.tile([P, ROW_TILES, P], BF16)
+        nc.vector.memset(coeff_cols[:], 0.0)
+
+        logits = keep.tile([P, ROW_TILES, EXPERTS], BF16)
+        nc.scalar.dma_start(out=logits[:], in_=logit_rows)
+        nc.scalar.dma_start(out=bias_rows[0:EXPERTS, :], in_=b0)
+        nc.scalar.dma_start(out=bias_rows[EXPERTS : 2 * EXPERTS, :], in_=b0)
+        x_sb = keep.tile([P, ROW_TILES, FEATURES], BF16)
+        for half in range(2):
+            tiles = slice(half * HALF, (half + 1) * HALF)
+            nc.sync.dma_start(out=x_sb[:, tiles, 0:LATENT], in_=z_rows[:, tiles, :])
+            nc.sync.dma_start(out=x_sb[:, tiles, LATENT:FEATURES], in_=c_rows[:, tiles, :])
+        w_raw = keep.tile([P, EXPERTS, PACK, HIDDEN], BF16)
+        for e in range(EXPERTS):
+            nc.sync.dma_start(out=w_raw[:, e], in_=w0[e].rearrange("(q t) h -> q t h", t=PACK))
+
+        per_tile = [P, ROW_TILES, EXPERTS]
+        top = keep.tile([P, ROW_TILES], F32)
+        nc.vector.tensor_reduce(out=top[:], in_=logits[:], axis=AXIS.X, op=ALU.max)
+        shifted = keep.tile(per_tile, F32)
+        nc.vector.tensor_tensor(
+            out=shifted[:], in0=logits[:], in1=top[:].unsqueeze(2).to_broadcast(per_tile), op=ALU.subtract
+        )
+        powers = keep.tile(per_tile, F32)
+        nc.scalar.activation(out=powers[:], in_=shifted[:], func=ACT.Exp)
+        total = keep.tile([P, ROW_TILES], F32)
+        nc.vector.tensor_reduce(out=total[:], in_=powers[:], axis=AXIS.X, op=ALU.add)
+        inv_total = keep.tile([P, ROW_TILES], F32)
+        nc.vector.reciprocal(out=inv_total[:], in_=total[:])
+        coeff = keep.tile(per_tile, F32)
+        nc.vector.tensor_tensor(
+            out=coeff[:], in0=powers[:], in1=inv_total[:].unsqueeze(2).to_broadcast(per_tile), op=ALU.mult
+        )
+
+        high = coeff_cols[:, :, 0:EXPERTS]
+        low = coeff_cols[:, :, EXPERTS : 2 * EXPERTS]
+        nc.vector.tensor_copy(out=high, in_=coeff[:])
+        nc.vector.tensor_tensor(out=low, in0=coeff[:], in1=high, op=ALU.subtract)
+        coeff_t_ps = psum_t.tile([P, ROW_TILES, P], BF16, tag="transposed")
+        for i in range(ROW_TILES):
+            nc.tensor.transpose(coeff_t_ps[:, i, :], coeff_cols[:, i, :], ident[:])
+        coeff_t = keep.tile([P, ROW_TILES, P], BF16)
+        nc.vector.tensor_copy(out=coeff_t[:], in_=coeff_t_ps[:])
+        acc = keep.tile([P, ROW_TILES, HIDDEN], F32)
+        for i in range(ROW_TILES):
+            product = product_pool(i).tile([P, HIDDEN], F32)
+            nc.tensor.matmul(out=product[:], lhsT=coeff_t[:, i, :], rhs=bias_rows[:], start=True, stop=True)
+            nc.scalar.copy(out=acc[:, i, :], in_=product[:])
+
+        stats = keep.tile([P, ROW_TILES, 6], F32)
+        mean_var = keep.tile([P, ROW_TILES, 2], F32)
+        std = keep.tile([P, ROW_TILES, 1], F32)
+        inv_std = keep.tile([P, ROW_TILES, 1], F32)
+        offset = keep.tile([P, ROW_TILES, 1], F32)
+        inp = keep.tile([P, ROW_TILES, PACK, P], BF16)
+        x_grouped = keep.tile([P, ROW_TILES * P * PACK], BF16, align_bytes=64)
+        x_codes = keep.tile([P, ROW_TILES * P], U32, align_bytes=64)
+        x_scales = keep.tile([P, ROW_TILES * P], U8, align_bytes=64)
+        for half in range(2):
+            tiles = slice(half * HALF, (half + 1) * HALF)
+            for i in range(half * HALF, (half + 1) * HALF):
+                nc.vector.bn_stats(out=stats[:, i, :], in_=x_sb[:, i, :])
+                nc.vector.bn_aggr(out=mean_var[:, i, :], in_=stats[:, i, :])
+            nc.scalar.activation(out=std[:, tiles, :], in_=mean_var[:, tiles, 1:2], func=ACT.Sqrt, bias=eps_col[:, 0:1])
+            nc.vector.reciprocal(out=inv_std[:, tiles, :], in_=std[:, tiles, :])
+            nc.vector.scalar_tensor_tensor(
+                out=offset[:, tiles, :], in0=mean_var[:, tiles, 0:1], scalar=-1.0, in1=inv_std[:, tiles, :],
+                op0=ALU.mult, op1=ALU.mult,
+            )
+            for first in range(half * HALF, (half + 1) * HALF, PAIR):
+                transposed = psum_t.tile([P, PAIR, PACK, P], BF16)
+                for n in range(PAIR):
+                    i = first + n
+                    nc.scalar.activation(
+                        out=inp[:, i], in_=x_sb[:, i, :].rearrange("r (q t) -> r t q", t=PACK),
+                        func=ACT.Identity, scale=inv_std[:, i, :], bias=offset[:, i, :],
+                    )
+                    for t in range(PACK):
+                        nc.tensor.transpose(transposed[:, n, t, :], inp[:, i, t, :], ident[:])
+                words = slice(first * P, (first + PAIR) * P)
+                values = slice(first * P * PACK, (first + PAIR) * P * PACK)
+                nc.vector.tensor_copy(
+                    out=x_grouped[:, values].rearrange("q (n r t) -> q n r t", n=PAIR, t=PACK),
+                    in_=transposed[:].rearrange("q n t r -> q n r t"),
+                )
+                nc.vector.quantize_mx(
+                    out=x_codes[:, words].bitcast(FP8X4), scales=x_scales[:, words], in_=x_grouped[:, values]
+                )
+
+        w_grouped = keep.tile([P, EXPERTS * HIDDEN * PACK], BF16, align_bytes=64)
+        w_codes = keep.tile([P, EXPERTS * HIDDEN], U32, align_bytes=64)
+        w_scales = keep.tile([P, EXPERTS * HIDDEN], U8, align_bytes=64)
+
+        def quantise_expert(e):
+            values = slice(e * HIDDEN * PACK, (e + 1) * HIDDEN * PACK)
+            nc.scalar.copy(
+                out=w_grouped[:, values].rearrange("q (g n t) -> q g t n", n=RUN, t=PACK),
+                in_=w_raw[:, e].rearrange("q t (g n) -> q g t n", n=RUN),
+            )
+            for start, width in ((0, WIDE), (WIDE, NARROW)):
+                words = slice(e * HIDDEN + start, e * HIDDEN + start + width)
+                values = slice((e * HIDDEN + start) * PACK, (e * HIDDEN + start + width) * PACK)
+                nc.vector.quantize_mx(
+                    out=w_codes[:, words].bitcast(FP8X4), scales=w_scales[:, words], in_=w_grouped[:, values]
+                )
+
+        def add_expert(e, i):
+            rows = slice(i * P, (i + 1) * P)
+            product = product_pool(i).tile([P, HIDDEN], F32)
+            for start, width in ((0, WIDE), (WIDE, NARROW)):
+                words = slice(e * HIDDEN + start, e * HIDDEN + start + width)
+                nc.tensor.matmul_mx(
+                    out=product[:, start : start + width],
+                    lhsT=x_codes[:, rows].bitcast(FP8X4), lhsT_scale=x_scales[:, rows],
+                    rhs=w_codes[:, words].bitcast(FP8X4), rhs_scale=w_scales[:, words],
+                    start=True, stop=True,
+                )
+            if in_scalar_team(i):
+                weighted = work.tile([P, HIDDEN], F32)
+                nc.scalar.activation(out=weighted[:], in_=product[:], func=ACT.Copy, scale=coeff[:, i, e : e + 1])
+                nc.gpsimd.tensor_tensor(out=acc[:, i, :], in0=acc[:, i, :], in1=weighted[:], op=ALU.add)
+            else:
+                nc.vector.scalar_tensor_tensor(
+                    out=acc[:, i, :], in0=product[:], scalar=coeff[:, i, e : e + 1], in1=acc[:, i, :],
+                    op0=ALU.mult, op1=ALU.add,
+                )
+
+        def elu_and_store(i):
+            grown = work.tile([P, HIDDEN], F32)
+            nc.scalar.activation(out=grown[:], in_=acc[:, i, :], func=ACT.Exp)
+            positive = work.tile([P, HIDDEN], F32)
+            nc.scalar.activation(out=positive[:], in_=acc[:, i, :], func=ACT.Relu)
+            result = work.tile([P, HIDDEN], F32)
+            nc.vector.scalar_tensor_tensor(
+                out=result[:], in0=grown[:], scalar=-1.0, in1=positive[:], op0=ALU.add, op1=ALU.min
+            )
+            nc.sync.dma_start(out=out_rows[:, i, :], in_=result[:])
+
+        quantise_expert(0)
+        for e in range(EXPERTS):
+            if e + 1 < EXPERTS:
+                quantise_expert(e + 1)
+            for i in range(ROW_TILES):
+                add_expert(e, i)
+                if e == EXPERTS - 1:
+                    elu_and_store(i)

@@ -17,7 +17,6 @@ PACK = 4
 ROWS, EXPERTS, LATENT, COND, HIDDEN = 1024, 8, 128, 384, 384
 FEATURES = LATENT + COND
 ROW_TILES = ROWS // P
-HALF = ROW_TILES // 2
 PAIR = 2
 EPS = 1e-5
 WIDE, NARROW = 256, 128
@@ -41,7 +40,7 @@ def tile_gatingmixeddecoder_pa_kernel(tc, z, c, gate_logits, w0, b0, out):
 
     with ExitStack() as ctx:
         keep = ctx.enter_context(tc.tile_pool(name="keep", bufs=1))
-        work = ctx.enter_context(tc.tile_pool(name="work", bufs=3))
+        work = ctx.enter_context(tc.tile_pool(name="work", bufs=4))
         psum_t = ctx.enter_context(tc.psum_pool(name="psum_t", bufs=2))
         psum_vector = ctx.enter_context(tc.psum_pool(name="psum_vector", bufs=3))
         psum_scalar = ctx.enter_context(tc.psum_pool(name="psum_scalar", bufs=3))
@@ -51,8 +50,8 @@ def tile_gatingmixeddecoder_pa_kernel(tc, z, c, gate_logits, w0, b0, out):
 
         ident = keep.tile([P, P], BF16)
         make_identity(nc, ident[:])
-        eps_col = keep.tile([P, 1], F32)
-        nc.vector.memset(eps_col[:], EPS)
+        minus_half = keep.tile([P, PAIR, 1], F32)
+        nc.vector.memset(minus_half[:], -0.5)
         bias_rows = keep.tile([P, HIDDEN], BF16)
         nc.vector.memset(bias_rows[:], 0.0)
         coeff_cols = keep.tile([P, ROW_TILES, P], BF16)
@@ -63,8 +62,8 @@ def tile_gatingmixeddecoder_pa_kernel(tc, z, c, gate_logits, w0, b0, out):
         nc.scalar.dma_start(out=bias_rows[0:EXPERTS, :], in_=b0)
         nc.scalar.dma_start(out=bias_rows[EXPERTS : 2 * EXPERTS, :], in_=b0)
         x_sb = keep.tile([P, ROW_TILES, FEATURES], BF16)
-        for half in range(2):
-            tiles = slice(half * HALF, (half + 1) * HALF)
+        for first in range(0, ROW_TILES, PAIR):
+            tiles = slice(first, first + PAIR)
             nc.sync.dma_start(out=x_sb[:, tiles, 0:LATENT], in_=z_rows[:, tiles, :])
             nc.sync.dma_start(out=x_sb[:, tiles, LATENT:FEATURES], in_=c_rows[:, tiles, :])
         w_raw = keep.tile([P, EXPERTS, PACK, HIDDEN], BF16)
@@ -97,7 +96,7 @@ def tile_gatingmixeddecoder_pa_kernel(tc, z, c, gate_logits, w0, b0, out):
         for i in range(ROW_TILES):
             nc.tensor.transpose(coeff_t_ps[:, i, :], coeff_cols[:, i, :], ident[:])
         coeff_t = keep.tile([P, ROW_TILES, P], BF16)
-        nc.vector.tensor_copy(out=coeff_t[:], in_=coeff_t_ps[:])
+        nc.scalar.copy(out=coeff_t[:], in_=coeff_t_ps[:])
         acc = keep.tile([P, ROW_TILES, HIDDEN], F32)
         for i in range(ROW_TILES):
             product = product_pool(i).tile([P, HIDDEN], F32)
@@ -106,43 +105,44 @@ def tile_gatingmixeddecoder_pa_kernel(tc, z, c, gate_logits, w0, b0, out):
 
         stats = keep.tile([P, ROW_TILES, 6], F32)
         mean_var = keep.tile([P, ROW_TILES, 2], F32)
-        std = keep.tile([P, ROW_TILES, 1], F32)
+        neg_mean = keep.tile([P, ROW_TILES, 1], F32)
+        var_eps = keep.tile([P, ROW_TILES, 1], F32)
         inv_std = keep.tile([P, ROW_TILES, 1], F32)
-        offset = keep.tile([P, ROW_TILES, 1], F32)
         inp = keep.tile([P, ROW_TILES, PACK, P], BF16)
         x_grouped = keep.tile([P, ROW_TILES * P * PACK], BF16, align_bytes=64)
         x_codes = keep.tile([P, ROW_TILES * P], U32, align_bytes=64)
         x_scales = keep.tile([P, ROW_TILES * P], U8, align_bytes=64)
-        for half in range(2):
-            tiles = slice(half * HALF, (half + 1) * HALF)
-            for i in range(half * HALF, (half + 1) * HALF):
+        for first in range(0, ROW_TILES, PAIR):
+            tiles = slice(first, first + PAIR)
+            for i in range(first, first + PAIR):
                 nc.vector.bn_stats(out=stats[:, i, :], in_=x_sb[:, i, :])
                 nc.vector.bn_aggr(out=mean_var[:, i, :], in_=stats[:, i, :])
-            nc.scalar.activation(out=std[:, tiles, :], in_=mean_var[:, tiles, 1:2], func=ACT.Sqrt, bias=eps_col[:, 0:1])
-            nc.vector.reciprocal(out=inv_std[:, tiles, :], in_=std[:, tiles, :])
-            nc.vector.scalar_tensor_tensor(
-                out=offset[:, tiles, :], in0=mean_var[:, tiles, 0:1], scalar=-1.0, in1=inv_std[:, tiles, :],
-                op0=ALU.mult, op1=ALU.mult,
+            nc.vector.tensor_scalar(
+                out=neg_mean[:, tiles, :], in0=mean_var[:, tiles, 0:1], scalar1=-1.0, scalar2=None, op0=ALU.mult
             )
-            for first in range(half * HALF, (half + 1) * HALF, PAIR):
-                transposed = psum_t.tile([P, PAIR, PACK, P], BF16)
-                for n in range(PAIR):
-                    i = first + n
-                    nc.scalar.activation(
-                        out=inp[:, i], in_=x_sb[:, i, :].rearrange("r (q t) -> r t q", t=PACK),
-                        func=ACT.Identity, scale=inv_std[:, i, :], bias=offset[:, i, :],
-                    )
-                    for t in range(PACK):
-                        nc.tensor.transpose(transposed[:, n, t, :], inp[:, i, t, :], ident[:])
-                words = slice(first * P, (first + PAIR) * P)
-                values = slice(first * P * PACK, (first + PAIR) * P * PACK)
-                nc.vector.tensor_copy(
-                    out=x_grouped[:, values].rearrange("q (n r t) -> q n r t", n=PAIR, t=PACK),
-                    in_=transposed[:].rearrange("q n t r -> q n r t"),
+            nc.vector.tensor_scalar(
+                out=var_eps[:, tiles, :], in0=mean_var[:, tiles, 1:2], scalar1=EPS, scalar2=None, op0=ALU.add
+            )
+            nc.gpsimd.tensor_tensor(out=inv_std[:, tiles, :], in0=var_eps[:, tiles, :], in1=minus_half[:], op=ALU.pow)
+            transposed = psum_t.tile([P, PAIR, PACK, P], BF16)
+            for n in range(PAIR):
+                i = first + n
+                engine = nc.vector if n == 0 else nc.gpsimd
+                engine.tensor_scalar(
+                    out=inp[:, i], in0=x_sb[:, i, :].rearrange("r (q t) -> r t q", t=PACK),
+                    scalar1=neg_mean[:, i, :], scalar2=inv_std[:, i, :], op0=ALU.add, op1=ALU.mult,
                 )
-                nc.vector.quantize_mx(
-                    out=x_codes[:, words].bitcast(FP8X4), scales=x_scales[:, words], in_=x_grouped[:, values]
-                )
+                for t in range(PACK):
+                    nc.tensor.transpose(transposed[:, n, t, :], inp[:, i, t, :], ident[:])
+            words = slice(first * P, (first + PAIR) * P)
+            values = slice(first * P * PACK, (first + PAIR) * P * PACK)
+            nc.scalar.copy(
+                out=x_grouped[:, values].rearrange("q (n r t) -> q n r t", n=PAIR, t=PACK),
+                in_=transposed[:].rearrange("q n t r -> q n r t"),
+            )
+            nc.vector.quantize_mx(
+                out=x_codes[:, words].bitcast(FP8X4), scales=x_scales[:, words], in_=x_grouped[:, values]
+            )
 
         w_grouped = keep.tile([P, EXPERTS * HIDDEN * PACK], BF16, align_bytes=64)
         w_codes = keep.tile([P, EXPERTS * HIDDEN], U32, align_bytes=64)
@@ -182,16 +182,23 @@ def tile_gatingmixeddecoder_pa_kernel(tc, z, c, gate_logits, w0, b0, out):
                     op0=ALU.mult, op1=ALU.add,
                 )
 
+        result = keep.tile([P, ROW_TILES, HIDDEN], F32)
+
         def elu_and_store(i):
             grown = work.tile([P, HIDDEN], F32)
             nc.scalar.activation(out=grown[:], in_=acc[:, i, :], func=ACT.Exp)
             positive = work.tile([P, HIDDEN], F32)
-            nc.scalar.activation(out=positive[:], in_=acc[:, i, :], func=ACT.Relu)
-            result = work.tile([P, HIDDEN], F32)
-            nc.vector.scalar_tensor_tensor(
-                out=result[:], in0=grown[:], scalar=-1.0, in1=positive[:], op0=ALU.add, op1=ALU.min
-            )
-            nc.sync.dma_start(out=out_rows[:, i, :], in_=result[:])
+            if in_scalar_team(i):
+                shrunk = work.tile([P, HIDDEN], F32)
+                nc.scalar.activation(out=shrunk[:], in_=grown[:], func=ACT.Relu, scale=-1.0, bias=1.0)
+                nc.scalar.activation(out=positive[:], in_=acc[:, i, :], func=ACT.Relu)
+                nc.gpsimd.tensor_tensor(out=result[:, i, :], in0=positive[:], in1=shrunk[:], op=ALU.subtract)
+            else:
+                nc.vector.tensor_scalar(out=positive[:], in0=acc[:, i, :], scalar1=0.0, scalar2=None, op0=ALU.max)
+                nc.vector.scalar_tensor_tensor(
+                    out=result[:, i, :], in0=grown[:], scalar=-1.0, in1=positive[:], op0=ALU.add, op1=ALU.min
+                )
+            nc.sync.dma_start(out=out_rows[:, i, :], in_=result[:, i, :])
 
         quantise_expert(0)
         for e in range(EXPERTS):

@@ -17,6 +17,7 @@ PACK = 4
 ROWS, EXPERTS, LATENT, COND, HIDDEN = 1024, 8, 128, 384, 384
 FEATURES = LATENT + COND
 ROW_TILES = ROWS // P
+PAIRS = ROW_TILES // 2
 PAIR = 2
 EPS = 1e-5
 WIDE, NARROW = 256, 128
@@ -62,13 +63,19 @@ def tile_gatingmixeddecoder_pa_kernel(tc, z, c, gate_logits, w0, b0, out):
         nc.scalar.dma_start(out=bias_rows[0:EXPERTS, :], in_=b0)
         nc.scalar.dma_start(out=bias_rows[EXPERTS : 2 * EXPERTS, :], in_=b0)
         x_sb = keep.tile([P, ROW_TILES, FEATURES], BF16)
+        w_raw = keep.tile([P, EXPERTS, PACK, HIDDEN], BF16)
+
+        def load_expert(e):
+            nc.sync.dma_start(out=w_raw[:, e], in_=w0[e].rearrange("(q t) h -> q t h", t=PACK))
+
         for first in range(0, ROW_TILES, PAIR):
             tiles = slice(first, first + PAIR)
             nc.sync.dma_start(out=x_sb[:, tiles, 0:LATENT], in_=z_rows[:, tiles, :])
             nc.sync.dma_start(out=x_sb[:, tiles, LATENT:FEATURES], in_=c_rows[:, tiles, :])
-        w_raw = keep.tile([P, EXPERTS, PACK, HIDDEN], BF16)
-        for e in range(EXPERTS):
-            nc.sync.dma_start(out=w_raw[:, e], in_=w0[e].rearrange("(q t) h -> q t h", t=PACK))
+            if first == 0:
+                load_expert(0)
+        for e in range(1, EXPERTS):
+            load_expert(e)
 
         per_tile = [P, ROW_TILES, EXPERTS]
         top = keep.tile([P, ROW_TILES], F32)
@@ -112,7 +119,8 @@ def tile_gatingmixeddecoder_pa_kernel(tc, z, c, gate_logits, w0, b0, out):
         x_grouped = keep.tile([P, ROW_TILES * P * PACK], BF16, align_bytes=64)
         x_codes = keep.tile([P, ROW_TILES * P], U32, align_bytes=64)
         x_scales = keep.tile([P, ROW_TILES * P], U8, align_bytes=64)
-        for first in range(0, ROW_TILES, PAIR):
+
+        def layer_norm_pair(first):
             tiles = slice(first, first + PAIR)
             for i in range(first, first + PAIR):
                 nc.vector.bn_stats(out=stats[:, i, :], in_=x_sb[:, i, :])
@@ -149,11 +157,12 @@ def tile_gatingmixeddecoder_pa_kernel(tc, z, c, gate_logits, w0, b0, out):
         w_scales = keep.tile([P, EXPERTS * HIDDEN], U8, align_bytes=64)
 
         def quantise_expert(e):
-            values = slice(e * HIDDEN * PACK, (e + 1) * HIDDEN * PACK)
-            nc.scalar.copy(
-                out=w_grouped[:, values].rearrange("q (g n t) -> q g t n", n=RUN, t=PACK),
-                in_=w_raw[:, e].rearrange("q t (g n) -> q g t n", n=RUN),
-            )
+            for start, width, copy in ((0, WIDE, nc.scalar.copy), (WIDE, NARROW, nc.vector.tensor_copy)):
+                values = slice((e * HIDDEN + start) * PACK, (e * HIDDEN + start + width) * PACK)
+                copy(
+                    out=w_grouped[:, values].rearrange("q (g n t) -> q g t n", n=RUN, t=PACK),
+                    in_=w_raw[:, e, :, start : start + width].rearrange("q t (g n) -> q g t n", n=RUN),
+                )
             for start, width in ((0, WIDE), (WIDE, NARROW)):
                 words = slice(e * HIDDEN + start, e * HIDDEN + start + width)
                 values = slice((e * HIDDEN + start) * PACK, (e * HIDDEN + start + width) * PACK)
@@ -200,11 +209,17 @@ def tile_gatingmixeddecoder_pa_kernel(tc, z, c, gate_logits, w0, b0, out):
                 )
             nc.sync.dma_start(out=out_rows[:, i, :], in_=result[:, i, :])
 
+        layer_norm_pair(0)
         quantise_expert(0)
-        for e in range(EXPERTS):
-            if e + 1 < EXPERTS:
-                quantise_expert(e + 1)
-            for i in range(ROW_TILES):
-                add_expert(e, i)
-                if e == EXPERTS - 1:
-                    elu_and_store(i)
+        for step in range(EXPERTS + PAIRS - 1):
+            if step + 1 < PAIRS:
+                layer_norm_pair((step + 1) * PAIR)
+            if step + 1 < EXPERTS:
+                quantise_expert(step + 1)
+            for j in range(PAIRS):
+                e = step - j
+                if 0 <= e < EXPERTS:
+                    for i in range(j * PAIR, (j + 1) * PAIR):
+                        add_expert(e, i)
+                        if e == EXPERTS - 1:
+                            elu_and_store(i)

@@ -17,13 +17,12 @@ PACK = 4
 ROWS, EXPERTS, LATENT, COND, HIDDEN = 1024, 8, 128, 384, 384
 FEATURES = LATENT + COND
 ROW_TILES = ROWS // P
-PAIRS = ROW_TILES // 2
 PAIR = 2
 EPS = 1e-5
 WIDE, NARROW = 256, 128
 RUN = 4
 
-SCALAR_TEAM_TILES = 3
+SCALAR_TEAM_TILES = 2
 
 FLOPS = 2 * ROWS * FEATURES * HIDDEN * EXPERTS
 
@@ -63,19 +62,13 @@ def tile_gatingmixeddecoder_pa_kernel(tc, z, c, gate_logits, w0, b0, out):
         nc.scalar.dma_start(out=bias_rows[0:EXPERTS, :], in_=b0)
         nc.scalar.dma_start(out=bias_rows[EXPERTS : 2 * EXPERTS, :], in_=b0)
         x_sb = keep.tile([P, ROW_TILES, FEATURES], BF16)
-        w_raw = keep.tile([P, EXPERTS, PACK, HIDDEN], BF16)
-
-        def load_expert(e):
-            nc.sync.dma_start(out=w_raw[:, e], in_=w0[e].rearrange("(q t) h -> q t h", t=PACK))
-
         for first in range(0, ROW_TILES, PAIR):
             tiles = slice(first, first + PAIR)
             nc.sync.dma_start(out=x_sb[:, tiles, 0:LATENT], in_=z_rows[:, tiles, :])
             nc.sync.dma_start(out=x_sb[:, tiles, LATENT:FEATURES], in_=c_rows[:, tiles, :])
-            if first == 0:
-                load_expert(0)
-        for e in range(1, EXPERTS):
-            load_expert(e)
+        w_raw = keep.tile([P, EXPERTS, PACK, HIDDEN], BF16)
+        for e in range(EXPERTS):
+            nc.sync.dma_start(out=w_raw[:, e], in_=w0[e].rearrange("(q t) h -> q t h", t=PACK))
 
         per_tile = [P, ROW_TILES, EXPERTS]
         top = keep.tile([P, ROW_TILES], F32)
@@ -119,8 +112,7 @@ def tile_gatingmixeddecoder_pa_kernel(tc, z, c, gate_logits, w0, b0, out):
         x_grouped = keep.tile([P, ROW_TILES * P * PACK], BF16, align_bytes=64)
         x_codes = keep.tile([P, ROW_TILES * P], U32, align_bytes=64)
         x_scales = keep.tile([P, ROW_TILES * P], U8, align_bytes=64)
-
-        def layer_norm_pair(first):
+        for first in range(0, ROW_TILES, PAIR):
             tiles = slice(first, first + PAIR)
             for i in range(first, first + PAIR):
                 nc.vector.bn_stats(out=stats[:, i, :], in_=x_sb[:, i, :])
@@ -157,12 +149,11 @@ def tile_gatingmixeddecoder_pa_kernel(tc, z, c, gate_logits, w0, b0, out):
         w_scales = keep.tile([P, EXPERTS * HIDDEN], U8, align_bytes=64)
 
         def quantise_expert(e):
-            for start, width, copy in ((0, WIDE, nc.scalar.copy), (WIDE, NARROW, nc.vector.tensor_copy)):
-                values = slice((e * HIDDEN + start) * PACK, (e * HIDDEN + start + width) * PACK)
-                copy(
-                    out=w_grouped[:, values].rearrange("q (g n t) -> q g t n", n=RUN, t=PACK),
-                    in_=w_raw[:, e, :, start : start + width].rearrange("q t (g n) -> q g t n", n=RUN),
-                )
+            values = slice(e * HIDDEN * PACK, (e + 1) * HIDDEN * PACK)
+            nc.scalar.copy(
+                out=w_grouped[:, values].rearrange("q (g n t) -> q g t n", n=RUN, t=PACK),
+                in_=w_raw[:, e].rearrange("q t (g n) -> q g t n", n=RUN),
+            )
             for start, width in ((0, WIDE), (WIDE, NARROW)):
                 words = slice(e * HIDDEN + start, e * HIDDEN + start + width)
                 values = slice((e * HIDDEN + start) * PACK, (e * HIDDEN + start + width) * PACK)
@@ -209,17 +200,11 @@ def tile_gatingmixeddecoder_pa_kernel(tc, z, c, gate_logits, w0, b0, out):
                 )
             nc.sync.dma_start(out=out_rows[:, i, :], in_=result[:, i, :])
 
-        layer_norm_pair(0)
         quantise_expert(0)
-        for step in range(EXPERTS + PAIRS - 1):
-            if step + 1 < PAIRS:
-                layer_norm_pair((step + 1) * PAIR)
-            if step + 1 < EXPERTS:
-                quantise_expert(step + 1)
-            for j in range(PAIRS):
-                e = step - j
-                if 0 <= e < EXPERTS:
-                    for i in range(j * PAIR, (j + 1) * PAIR):
-                        add_expert(e, i)
-                        if e == EXPERTS - 1:
-                            elu_and_store(i)
+        for e in range(EXPERTS):
+            if e + 1 < EXPERTS:
+                quantise_expert(e + 1)
+            for i in range(ROW_TILES):
+                add_expert(e, i)
+                if e == EXPERTS - 1:
+                    elu_and_store(i)

@@ -50,6 +50,8 @@ def tile_gatingmixeddecoder_pa_kernel(tc, z, c, gate_logits, w0, b0, out):
 
         ident = keep.tile([P, P], BF16)
         make_identity(nc, ident[:])
+        ident_f32 = keep.tile([P, P], F32)
+        make_identity(nc, ident_f32[:])
         minus_half = keep.tile([P, PAIR, 1], F32)
         nc.vector.memset(minus_half[:], -0.5)
         bias_rows = keep.tile([P, HIDDEN], BF16)
@@ -99,9 +101,10 @@ def tile_gatingmixeddecoder_pa_kernel(tc, z, c, gate_logits, w0, b0, out):
         nc.scalar.copy(out=coeff_t[:], in_=coeff_t_ps[:])
         acc = keep.tile([P, ROW_TILES, HIDDEN], F32)
         for i in range(ROW_TILES):
-            product = product_pool(i).tile([P, HIDDEN], F32)
-            nc.tensor.matmul(out=product[:], lhsT=coeff_t[:, i, :], rhs=bias_rows[:], start=True, stop=True)
-            nc.scalar.copy(out=acc[:, i, :], in_=product[:])
+            if not in_scalar_team(i):
+                product = product_pool(i).tile([P, HIDDEN], F32)
+                nc.tensor.matmul(out=product[:], lhsT=coeff_t[:, i, :], rhs=bias_rows[:], start=True, stop=True)
+                nc.scalar.copy(out=acc[:, i, :], in_=product[:])
 
         stats = keep.tile([P, ROW_TILES, 6], F32)
         mean_var = keep.tile([P, ROW_TILES, 2], F32)
@@ -161,6 +164,9 @@ def tile_gatingmixeddecoder_pa_kernel(tc, z, c, gate_logits, w0, b0, out):
                     out=w_codes[:, words].bitcast(FP8X4), scales=w_scales[:, words], in_=w_grouped[:, values]
                 )
 
+        turned_sums = {}
+        BLOCKS = HIDDEN // P
+
         def add_expert(e, i):
             rows = slice(i * P, (i + 1) * P)
             product = product_pool(i).tile([P, HIDDEN], F32)
@@ -175,7 +181,15 @@ def tile_gatingmixeddecoder_pa_kernel(tc, z, c, gate_logits, w0, b0, out):
             if in_scalar_team(i):
                 weighted = work.tile([P, HIDDEN], F32)
                 nc.scalar.activation(out=weighted[:], in_=product[:], func=ACT.Copy, scale=coeff[:, i, e : e + 1])
-                nc.gpsimd.tensor_tensor(out=acc[:, i, :], in0=acc[:, i, :], in1=weighted[:], op=ALU.add)
+                if e == 0:
+                    turned = psum_t.tile([P, BLOCKS, P], F32, tag="transposed")
+                    turned_sums[i] = turned
+                turned = turned_sums[i]
+                for b in range(BLOCKS):
+                    nc.tensor.matmul(
+                        out=turned[:, b, :], lhsT=weighted[:, b * P : (b + 1) * P], rhs=ident_f32[:], is_transpose=True,
+                        start=(e == 0 and b == 0), stop=(e == EXPERTS - 1 and b == BLOCKS - 1),
+                    )
             else:
                 nc.vector.scalar_tensor_tensor(
                     out=acc[:, i, :], in0=product[:], scalar=coeff[:, i, e : e + 1], in1=acc[:, i, :],
@@ -186,14 +200,25 @@ def tile_gatingmixeddecoder_pa_kernel(tc, z, c, gate_logits, w0, b0, out):
 
         def elu_and_store(i):
             grown = work.tile([P, HIDDEN], F32)
-            nc.scalar.activation(out=grown[:], in_=acc[:, i, :], func=ACT.Exp)
-            positive = work.tile([P, HIDDEN], F32)
             if in_scalar_team(i):
+                turned_sb = work.tile([P, BLOCKS, P], F32)
+                nc.scalar.copy(out=turned_sb[:], in_=turned_sums[i][:])
+                total_ps = psum_scalar.tile([P, HIDDEN], F32, tag="product")
+                nc.tensor.matmul(out=total_ps[:], lhsT=coeff_t[:, i, :], rhs=bias_rows[:], start=True, stop=False)
+                for b in range(BLOCKS):
+                    nc.tensor.matmul(
+                        out=total_ps[:, b * P : (b + 1) * P], lhsT=turned_sb[:, b, :], rhs=ident_f32[:], is_transpose=True,
+                        start=False, stop=(b == BLOCKS - 1),
+                    )
+                nc.scalar.activation(out=grown[:], in_=total_ps[:], func=ACT.Exp)
                 shrunk = work.tile([P, HIDDEN], F32)
                 nc.scalar.activation(out=shrunk[:], in_=grown[:], func=ACT.Relu, scale=-1.0, bias=1.0)
-                nc.scalar.activation(out=positive[:], in_=acc[:, i, :], func=ACT.Relu)
-                nc.gpsimd.tensor_tensor(out=result[:, i, :], in0=positive[:], in1=shrunk[:], op=ALU.subtract)
+                nc.vector.scalar_tensor_tensor(
+                    out=result[:, i, :], in0=shrunk[:], scalar=-1.0, in1=total_ps[:], op0=ALU.mult, op1=ALU.max
+                )
             else:
+                nc.scalar.activation(out=grown[:], in_=acc[:, i, :], func=ACT.Exp)
+                positive = work.tile([P, HIDDEN], F32)
                 nc.vector.tensor_scalar(out=positive[:], in0=acc[:, i, :], scalar1=0.0, scalar2=None, op0=ALU.max)
                 nc.vector.scalar_tensor_tensor(
                     out=result[:, i, :], in0=grown[:], scalar=-1.0, in1=positive[:], op0=ALU.add, op1=ALU.min

@@ -18,6 +18,7 @@ ROWS, EXPERTS, LATENT, COND, HIDDEN = 1024, 8, 128, 384, 384
 FEATURES = LATENT + COND
 ROW_TILES = ROWS // P
 PAIR = 2
+HALVES = 2
 EPS = 1e-5
 WIDE, NARROW = 256, 128
 RUN = 4
@@ -70,7 +71,10 @@ def tile_gatingmixeddecoder_pa_kernel(tc, z, c, gate_logits, w0, b0, out):
             nc.sync.dma_start(out=x_sb[:, tiles, LATENT:FEATURES], in_=c_rows[:, tiles, :])
         w_raw = keep.tile([P, EXPERTS, PACK, HIDDEN], BF16)
         for e in range(EXPERTS):
-            nc.sync.dma_start(out=w_raw[:, e], in_=w0[e].rearrange("(q t) h -> q t h", t=PACK))
+            nc.sync.dma_start(
+                out=w_raw[:, e].rearrange("q (u s) h -> q u (s h)", u=HALVES),
+                in_=w0[e].rearrange("(u q s) h -> q u (s h)", u=HALVES, s=PACK // HALVES),
+            )
 
         per_tile = [P, ROW_TILES, EXPERTS]
         top = keep.tile([P, ROW_TILES], F32)
@@ -108,10 +112,9 @@ def tile_gatingmixeddecoder_pa_kernel(tc, z, c, gate_logits, w0, b0, out):
 
         stats = keep.tile([P, ROW_TILES, 6], F32)
         mean_var = keep.tile([P, ROW_TILES, 2], F32)
-        neg_mean = keep.tile([P, ROW_TILES, 1], F32)
         var_eps = keep.tile([P, ROW_TILES, 1], F32)
         inv_std = keep.tile([P, ROW_TILES, 1], F32)
-        inp = keep.tile([P, ROW_TILES, PACK, P], BF16)
+        inp = keep.tile([P, ROW_TILES, FEATURES], BF16)
         x_grouped = keep.tile([P, ROW_TILES * P * PACK], BF16, align_bytes=64)
         x_codes = keep.tile([P, ROW_TILES * P], U32, align_bytes=64)
         x_scales = keep.tile([P, ROW_TILES * P], U8, align_bytes=64)
@@ -121,27 +124,24 @@ def tile_gatingmixeddecoder_pa_kernel(tc, z, c, gate_logits, w0, b0, out):
                 nc.vector.bn_stats(out=stats[:, i, :], in_=x_sb[:, i, :])
                 nc.vector.bn_aggr(out=mean_var[:, i, :], in_=stats[:, i, :])
             nc.vector.tensor_scalar(
-                out=neg_mean[:, tiles, :], in0=mean_var[:, tiles, 0:1], scalar1=-1.0, scalar2=None, op0=ALU.mult
-            )
-            nc.vector.tensor_scalar(
                 out=var_eps[:, tiles, :], in0=mean_var[:, tiles, 1:2], scalar1=EPS, scalar2=None, op0=ALU.add
             )
             nc.gpsimd.tensor_tensor(out=inv_std[:, tiles, :], in0=var_eps[:, tiles, :], in1=minus_half[:], op=ALU.pow)
-            transposed = psum_t.tile([P, PAIR, PACK, P], BF16)
+            transposed = psum_t.tile([P, PAIR, HALVES, P], F32)
             for n in range(PAIR):
                 i = first + n
-                engine = nc.vector if n == 0 else nc.gpsimd
-                engine.tensor_scalar(
-                    out=inp[:, i], in0=x_sb[:, i, :].rearrange("r (q t) -> r t q", t=PACK),
-                    scalar1=neg_mean[:, i, :], scalar2=inv_std[:, i, :], op0=ALU.add, op1=ALU.mult,
+                nc.vector.tensor_scalar(
+                    out=inp[:, i, :], in0=x_sb[:, i, :],
+                    scalar1=mean_var[:, i, 0:1], scalar2=inv_std[:, i, :], op0=ALU.subtract, op1=ALU.mult,
                 )
-                for t in range(PACK):
-                    nc.tensor.transpose(transposed[:, n, t, :], inp[:, i, t, :], ident[:])
+                words_of_row = inp[:, i, :].bitcast(F32)
+                for u in range(HALVES):
+                    nc.tensor.transpose(transposed[:, n, u, :], words_of_row[:, u * P : (u + 1) * P], ident_f32[:])
             words = slice(first * P, (first + PAIR) * P)
             values = slice(first * P * PACK, (first + PAIR) * P * PACK)
             nc.scalar.copy(
-                out=x_grouped[:, values].rearrange("q (n r t) -> q n r t", n=PAIR, t=PACK),
-                in_=transposed[:].rearrange("q n t r -> q n r t"),
+                out=x_grouped[:, values].bitcast(F32).rearrange("q (n r u) -> q n r u", n=PAIR, u=HALVES),
+                in_=transposed[:].rearrange("q n u r -> q n r u"),
             )
             nc.vector.quantize_mx(
                 out=x_codes[:, words].bitcast(FP8X4), scales=x_scales[:, words], in_=x_grouped[:, values]

@@ -18,6 +18,7 @@ ROWS, EXPERTS, LATENT, COND, HIDDEN = 1024, 8, 128, 384, 384
 FEATURES = LATENT + COND
 ROW_TILES = ROWS // P
 PAIR = 2
+SCALAR_STATS_PAIRS = ()
 HALVES = 2
 EPS = 1e-5
 WIDE, NARROW = 256, 128
@@ -43,8 +44,8 @@ def tile_gatingmixeddecoder_pa_kernel(tc, z, c, gate_logits, w0, b0, out):
         keep = ctx.enter_context(tc.tile_pool(name="keep", bufs=1))
         work = ctx.enter_context(tc.tile_pool(name="work", bufs=4))
         psum_t = ctx.enter_context(tc.psum_pool(name="psum_t", bufs=2))
-        psum_vector = ctx.enter_context(tc.psum_pool(name="psum_vector", bufs=3))
-        psum_scalar = ctx.enter_context(tc.psum_pool(name="psum_scalar", bufs=3))
+        psum_vector = ctx.enter_context(tc.psum_pool(name="psum_products", bufs=6))
+        psum_scalar = psum_vector
 
         def product_pool(i):
             return psum_scalar if in_scalar_team(i) else psum_vector
@@ -65,8 +66,7 @@ def tile_gatingmixeddecoder_pa_kernel(tc, z, c, gate_logits, w0, b0, out):
         nc.scalar.dma_start(out=bias_rows[0:EXPERTS, :], in_=b0)
         nc.scalar.dma_start(out=bias_rows[EXPERTS : 2 * EXPERTS, :], in_=b0)
         x_sb = keep.tile([P, ROW_TILES, FEATURES], BF16)
-        for first in range(0, ROW_TILES, PAIR):
-            tiles = slice(first, first + PAIR)
+        for tiles in (slice(0, 1), slice(1, 2), slice(2, 4), slice(4, 6), slice(6, 8)):
             nc.sync.dma_start(out=x_sb[:, tiles, 0:LATENT], in_=z_rows[:, tiles, :])
             nc.sync.dma_start(out=x_sb[:, tiles, LATENT:FEATURES], in_=c_rows[:, tiles, :])
         w_raw = keep.tile([P, EXPERTS, PACK, HIDDEN], BF16)
@@ -118,14 +118,35 @@ def tile_gatingmixeddecoder_pa_kernel(tc, z, c, gate_logits, w0, b0, out):
         x_grouped = keep.tile([P, ROW_TILES * P * PACK], BF16, align_bytes=64)
         x_codes = keep.tile([P, ROW_TILES * P], U32, align_bytes=64)
         x_scales = keep.tile([P, ROW_TILES * P], U8, align_bytes=64)
+        sums = keep.tile([P, ROW_TILES, 2], F32)
+        for p in SCALAR_STATS_PAIRS:
+            tiles = slice(p * PAIR, (p + 1) * PAIR)
+            for i in range(p * PAIR, (p + 1) * PAIR):
+                scrap = work.tile([P, FEATURES], BF16)
+                nc.scalar.activation(out=scrap[:], in_=x_sb[:, i, :], func=ACT.Copy, accum_out=sums[:, i, 0:1])
+            nc.vector.tensor_scalar(
+                out=mean_var[:, tiles, 0:1], in0=sums[:, tiles, 0:1], scalar1=1.0 / FEATURES, scalar2=None, op0=ALU.mult
+            )
+            for i in range(p * PAIR, (p + 1) * PAIR):
+                scrap = work.tile([P, FEATURES], BF16)
+                nc.scalar.activation(
+                    out=scrap[:], in_=x_sb[:, i, :], func=ACT.Square, scale=-1.0, bias=mean_var[:, i, 0:1],
+                    accum_out=sums[:, i, 1:2],
+                )
         for first in range(0, ROW_TILES, PAIR):
             tiles = slice(first, first + PAIR)
-            for i in range(first, first + PAIR):
-                nc.vector.bn_stats(out=stats[:, i, :], in_=x_sb[:, i, :])
-                nc.vector.bn_aggr(out=mean_var[:, i, :], in_=stats[:, i, :])
-            nc.vector.tensor_scalar(
-                out=var_eps[:, tiles, :], in0=mean_var[:, tiles, 1:2], scalar1=EPS, scalar2=None, op0=ALU.add
-            )
+            if first // PAIR in SCALAR_STATS_PAIRS:
+                nc.vector.tensor_scalar(
+                    out=var_eps[:, tiles, :], in0=sums[:, tiles, 1:2], scalar1=1.0 / FEATURES, scalar2=EPS,
+                    op0=ALU.mult, op1=ALU.add,
+                )
+            else:
+                for i in range(first, first + PAIR):
+                    nc.vector.bn_stats(out=stats[:, i, :], in_=x_sb[:, i, :])
+                    nc.vector.bn_aggr(out=mean_var[:, i, :], in_=stats[:, i, :])
+                nc.vector.tensor_scalar(
+                    out=var_eps[:, tiles, :], in0=mean_var[:, tiles, 1:2], scalar1=EPS, scalar2=None, op0=ALU.add
+                )
             nc.gpsimd.tensor_tensor(out=inv_std[:, tiles, :], in0=var_eps[:, tiles, :], in1=minus_half[:], op=ALU.pow)
             transposed = psum_t.tile([P, PAIR, HALVES, P], F32)
             for n in range(PAIR):
@@ -151,13 +172,15 @@ def tile_gatingmixeddecoder_pa_kernel(tc, z, c, gate_logits, w0, b0, out):
         w_codes = keep.tile([P, EXPERTS * HIDDEN], U32, align_bytes=64)
         w_scales = keep.tile([P, EXPERTS * HIDDEN], U8, align_bytes=64)
 
-        def quantise_expert(e):
+        def regroup_expert(e):
             values = slice(e * HIDDEN * PACK, (e + 1) * HIDDEN * PACK)
             nc.scalar.copy(
                 out=w_grouped[:, values].rearrange("q (g n t) -> q g t n", n=RUN, t=PACK),
                 in_=w_raw[:, e].rearrange("q t (g n) -> q g t n", n=RUN),
             )
-            for start, width in ((0, WIDE), (WIDE, NARROW)):
+
+        def quantise_experts(e, count):
+            for start, width in ((0, count * WIDE), (count * WIDE, count * NARROW)):
                 words = slice(e * HIDDEN + start, e * HIDDEN + start + width)
                 values = slice((e * HIDDEN + start) * PACK, (e * HIDDEN + start + width) * PACK)
                 nc.vector.quantize_mx(
@@ -225,11 +248,16 @@ def tile_gatingmixeddecoder_pa_kernel(tc, z, c, gate_logits, w0, b0, out):
                 )
             nc.sync.dma_start(out=out_rows[:, i, :], in_=result[:, i, :])
 
-        quantise_expert(0)
+        regroup_expert(0)
+        quantise_experts(0, 1)
+        regroup_expert(1)
+        quantise_experts(1, 1)
         for e in range(EXPERTS):
-            if e + 1 < EXPERTS:
-                quantise_expert(e + 1)
+            if e + 2 < EXPERTS:
+                regroup_expert(e + 2)
             for i in range(ROW_TILES):
                 add_expert(e, i)
                 if e == EXPERTS - 1:
                     elu_and_store(i)
+                if i == ROW_TILES // 2 - 1 and e % 2 == 1 and e + 2 < EXPERTS:
+                    quantise_experts(e + 1, 2)

@@ -173,11 +173,13 @@ def tile_gatingmixeddecoder_pa_kernel(tc, z, c, gate_logits, w0, b0, out):
         w_scales = keep.tile([P, EXPERTS * HIDDEN], U8, align_bytes=64)
 
         def regroup_expert(e):
-            values = slice(e * HIDDEN * PACK, (e + 1) * HIDDEN * PACK)
-            nc.scalar.copy(
-                out=w_grouped[:, values].rearrange("q (g n t) -> q g t n", n=RUN, t=PACK),
-                in_=w_raw[:, e].rearrange("q t (g n) -> q g t n", n=RUN),
-            )
+            for piece in range(HIDDEN // P):
+                columns = slice(piece * P, (piece + 1) * P)
+                values = slice((e * HIDDEN + piece * P) * PACK, (e * HIDDEN + (piece + 1) * P) * PACK)
+                nc.scalar.copy(
+                    out=w_grouped[:, values].rearrange("q (g n t) -> q g t n", n=RUN, t=PACK),
+                    in_=w_raw[:, e, :, columns].rearrange("q t (g n) -> q g t n", n=RUN),
+                )
 
         def quantise_experts(e, count):
             for start, width in ((0, count * WIDE), (count * WIDE, count * NARROW)):

from contextlib import ExitStack

import concourse.mybir as mybir
from concourse.masks import make_identity

F32 = mybir.dt.float32
BF16 = mybir.dt.bfloat16
U32 = mybir.dt.uint32
U8 = mybir.dt.uint8
FP8X4 = mybir.dt.float8_e4m3fn_x4
ALU = mybir.AluOpType
ACT = mybir.ActivationFunctionType
AXIS = mybir.AxisListType

P = 128
PACK = 4
ROWS, EXPERTS, LATENT, COND, HIDDEN = 1024, 8, 128, 384, 384
FEATURES = LATENT + COND
ROW_TILES = ROWS // P
PAIR = 2
SCALAR_STATS_PAIRS = ()
HALVES = 2
EPS = 1e-5
WIDE, NARROW = 256, 128
RUN = 4

SCALAR_TEAM_TILES = 2

FLOPS = 2 * ROWS * FEATURES * HIDDEN * EXPERTS


def in_scalar_team(i):
    return i % 2 == 1 and i // 2 < SCALAR_TEAM_TILES


def tile_gatingmixeddecoder_pa_kernel(tc, z, c, gate_logits, w0, b0, out):
    nc = tc.nc
    z_rows = z.rearrange("(p i) f -> p i f", i=ROW_TILES)
    c_rows = c.rearrange("(p i) f -> p i f", i=ROW_TILES)
    logit_rows = gate_logits.rearrange("(p i) e -> p i e", i=ROW_TILES)
    out_rows = out.rearrange("(p i) h -> p i h", i=ROW_TILES)

    with ExitStack() as ctx:
        keep = ctx.enter_context(tc.tile_pool(name="keep", bufs=1))
        work = ctx.enter_context(tc.tile_pool(name="work", bufs=4))
        psum_t = ctx.enter_context(tc.psum_pool(name="psum_t", bufs=2))
        psum_vector = ctx.enter_context(tc.psum_pool(name="psum_products", bufs=6))
        psum_scalar = psum_vector

        def product_pool(i):
            return psum_scalar if in_scalar_team(i) else psum_vector

        ident = keep.tile([P, P], BF16)
        make_identity(nc, ident[:])
        ident_f32 = keep.tile([P, P], F32)
        make_identity(nc, ident_f32[:])
        minus_half = keep.tile([P, PAIR, 1], F32)
        nc.vector.memset(minus_half[:], -0.5)
        bias_rows = keep.tile([P, HIDDEN], BF16)
        nc.vector.memset(bias_rows[:], 0.0)
        coeff_cols = keep.tile([P, ROW_TILES, P], BF16)
        nc.vector.memset(coeff_cols[:], 0.0)

        logits = keep.tile([P, ROW_TILES, EXPERTS], BF16)
        nc.scalar.dma_start(out=logits[:], in_=logit_rows)
        nc.scalar.dma_start(out=bias_rows[0:EXPERTS, :], in_=b0)
        nc.scalar.dma_start(out=bias_rows[EXPERTS : 2 * EXPERTS, :], in_=b0)
        x_sb = keep.tile([P, ROW_TILES, FEATURES], BF16)
        for tiles in (slice(0, 1), slice(1, 2), slice(2, 4), slice(4, 6), slice(6, 8)):
            nc.sync.dma_start(out=x_sb[:, tiles, 0:LATENT], in_=z_rows[:, tiles, :])
            nc.sync.dma_start(out=x_sb[:, tiles, LATENT:FEATURES], in_=c_rows[:, tiles, :])
        w_raw = keep.tile([P, EXPERTS, PACK, HIDDEN], BF16)
        for e in range(EXPERTS):
            nc.sync.dma_start(
                out=w_raw[:, e].rearrange("q (u s) h -> q u (s h)", u=HALVES),
                in_=w0[e].rearrange("(u q s) h -> q u (s h)", u=HALVES, s=PACK // HALVES),
            )

        per_tile = [P, ROW_TILES, EXPERTS]
        top = keep.tile([P, ROW_TILES], F32)
        nc.vector.tensor_reduce(out=top[:], in_=logits[:], axis=AXIS.X, op=ALU.max)
        shifted = keep.tile(per_tile, F32)
        nc.vector.tensor_tensor(
            out=shifted[:], in0=logits[:], in1=top[:].unsqueeze(2).to_broadcast(per_tile), op=ALU.subtract
        )
        powers = keep.tile(per_tile, F32)
        nc.scalar.activation(out=powers[:], in_=shifted[:], func=ACT.Exp)
        total = keep.tile([P, ROW_TILES], F32)
        nc.vector.tensor_reduce(out=total[:], in_=powers[:], axis=AXIS.X, op=ALU.add)
        inv_total = keep.tile([P, ROW_TILES], F32)
        nc.vector.reciprocal(out=inv_total[:], in_=total[:])
        coeff = keep.tile(per_tile, F32)
        nc.vector.tensor_tensor(
            out=coeff[:], in0=powers[:], in1=inv_total[:].unsqueeze(2).to_broadcast(per_tile), op=ALU.mult
        )

        high = coeff_cols[:, :, 0:EXPERTS]
        low = coeff_cols[:, :, EXPERTS : 2 * EXPERTS]
        nc.vector.tensor_copy(out=high, in_=coeff[:])
        nc.vector.tensor_tensor(out=low, in0=coeff[:], in1=high, op=ALU.subtract)
        coeff_t_ps = psum_t.tile([P, ROW_TILES, P], BF16, tag="transposed")
        for i in range(ROW_TILES):
            nc.tensor.transpose(coeff_t_ps[:, i, :], coeff_cols[:, i, :], ident[:])
        coeff_t = keep.tile([P, ROW_TILES, P], BF16)
        nc.scalar.copy(out=coeff_t[:], in_=coeff_t_ps[:])
        acc = keep.tile([P, ROW_TILES, HIDDEN], F32)
        for i in range(ROW_TILES):
            if not in_scalar_team(i):
                product = product_pool(i).tile([P, HIDDEN], F32)
                nc.tensor.matmul(out=product[:], lhsT=coeff_t[:, i, :], rhs=bias_rows[:], start=True, stop=True)
                nc.scalar.copy(out=acc[:, i, :], in_=product[:])

        stats = keep.tile([P, ROW_TILES, 6], F32)
        mean_var = keep.tile([P, ROW_TILES, 2], F32)
        var_eps = keep.tile([P, ROW_TILES, 1], F32)
        inv_std = keep.tile([P, ROW_TILES, 1], F32)
        inp = keep.tile([P, ROW_TILES, FEATURES], BF16)
        x_grouped = keep.tile([P, ROW_TILES * P * PACK], BF16, align_bytes=64)
        x_codes = keep.tile([P, ROW_TILES * P], U32, align_bytes=64)
        x_scales = keep.tile([P, ROW_TILES * P], U8, align_bytes=64)
        sums = keep.tile([P, ROW_TILES, 2], F32)
        for p in SCALAR_STATS_PAIRS:
            tiles = slice(p * PAIR, (p + 1) * PAIR)
            for i in range(p * PAIR, (p + 1) * PAIR):
                scrap = work.tile([P, FEATURES], BF16)
                nc.scalar.activation(out=scrap[:], in_=x_sb[:, i, :], func=ACT.Copy, accum_out=sums[:, i, 0:1])
            nc.vector.tensor_scalar(
                out=mean_var[:, tiles, 0:1], in0=sums[:, tiles, 0:1], scalar1=1.0 / FEATURES, scalar2=None, op0=ALU.mult
            )
            for i in range(p * PAIR, (p + 1) * PAIR):
                scrap = work.tile([P, FEATURES], BF16)
                nc.scalar.activation(
                    out=scrap[:], in_=x_sb[:, i, :], func=ACT.Square, scale=-1.0, bias=mean_var[:, i, 0:1],
                    accum_out=sums[:, i, 1:2],
                )
        for first in range(0, ROW_TILES, PAIR):
            tiles = slice(first, first + PAIR)
            if first // PAIR in SCALAR_STATS_PAIRS:
                nc.vector.tensor_scalar(
                    out=var_eps[:, tiles, :], in0=sums[:, tiles, 1:2], scalar1=1.0 / FEATURES, scalar2=EPS,
                    op0=ALU.mult, op1=ALU.add,
                )
            else:
                for i in range(first, first + PAIR):
                    nc.vector.bn_stats(out=stats[:, i, :], in_=x_sb[:, i, :])
                    nc.vector.bn_aggr(out=mean_var[:, i, :], in_=stats[:, i, :])
                nc.vector.tensor_scalar(
                    out=var_eps[:, tiles, :], in0=mean_var[:, tiles, 1:2], scalar1=EPS, scalar2=None, op0=ALU.add
                )
            nc.gpsimd.tensor_tensor(out=inv_std[:, tiles, :], in0=var_eps[:, tiles, :], in1=minus_half[:], op=ALU.pow)
            transposed = psum_t.tile([P, PAIR, HALVES, P], F32)
            for n in range(PAIR):
                i = first + n
                nc.vector.tensor_scalar(
                    out=inp[:, i, :], in0=x_sb[:, i, :],
                    scalar1=mean_var[:, i, 0:1], scalar2=inv_std[:, i, :], op0=ALU.subtract, op1=ALU.mult,
                )
                words_of_row = inp[:, i, :].bitcast(F32)
                for u in range(HALVES):
                    nc.tensor.transpose(transposed[:, n, u, :], words_of_row[:, u * P : (u + 1) * P], ident_f32[:])
            words = slice(first * P, (first + PAIR) * P)
            values = slice(first * P * PACK, (first + PAIR) * P * PACK)
            nc.scalar.copy(
                out=x_grouped[:, values].bitcast(F32).rearrange("q (n r u) -> q n r u", n=PAIR, u=HALVES),
                in_=transposed[:].rearrange("q n u r -> q n r u"),
            )
            nc.vector.quantize_mx(
                out=x_codes[:, words].bitcast(FP8X4), scales=x_scales[:, words], in_=x_grouped[:, values]
            )

        w_grouped = keep.tile([P, EXPERTS * HIDDEN * PACK], BF16, align_bytes=64)
        w_codes = keep.tile([P, EXPERTS * HIDDEN], U32, align_bytes=64)
        w_scales = keep.tile([P, EXPERTS * HIDDEN], U8, align_bytes=64)

        def regroup_expert(e):
            for piece in range(HIDDEN // P):
                columns = slice(piece * P, (piece + 1) * P)
                values = slice((e * HIDDEN + piece * P) * PACK, (e * HIDDEN + (piece + 1) * P) * PACK)
                nc.scalar.copy(
                    out=w_grouped[:, values].rearrange("q (g n t) -> q g t n", n=RUN, t=PACK),
                    in_=w_raw[:, e, :, columns].rearrange("q t (g n) -> q g t n", n=RUN),
                )

        def quantise_experts(e, count):
            for start, width in ((0, count * WIDE), (count * WIDE, count * NARROW)):
                words = slice(e * HIDDEN + start, e * HIDDEN + start + width)
                values = slice((e * HIDDEN + start) * PACK, (e * HIDDEN + start + width) * PACK)
                nc.vector.quantize_mx(
                    out=w_codes[:, words].bitcast(FP8X4), scales=w_scales[:, words], in_=w_grouped[:, values]
                )

        turned_sums = {}
        BLOCKS = HIDDEN // P

        def add_expert(e, i):
            rows = slice(i * P, (i + 1) * P)
            product = product_pool(i).tile([P, HIDDEN], F32)
            for start, width in ((0, WIDE), (WIDE, NARROW)):
                words = slice(e * HIDDEN + start, e * HIDDEN + start + width)
                nc.tensor.matmul_mx(
                    out=product[:, start : start + width],
                    lhsT=x_codes[:, rows].bitcast(FP8X4), lhsT_scale=x_scales[:, rows],
                    rhs=w_codes[:, words].bitcast(FP8X4), rhs_scale=w_scales[:, words],
                    start=True, stop=True,
                )
            if in_scalar_team(i):
                weighted = work.tile([P, HIDDEN], F32)
                nc.scalar.activation(out=weighted[:], in_=product[:], func=ACT.Copy, scale=coeff[:, i, e : e + 1])
                if e == 0:
                    turned = psum_t.tile([P, BLOCKS, P], F32, tag="transposed")
                    turned_sums[i] = turned
                turned = turned_sums[i]
                for b in range(BLOCKS):
                    nc.tensor.matmul(
                        out=turned[:, b, :], lhsT=weighted[:, b * P : (b + 1) * P], rhs=ident_f32[:], is_transpose=True,
                        start=(e == 0 and b == 0), stop=(e == EXPERTS - 1 and b == BLOCKS - 1),
                    )
            else:
                nc.vector.scalar_tensor_tensor(
                    out=acc[:, i, :], in0=product[:], scalar=coeff[:, i, e : e + 1], in1=acc[:, i, :],
                    op0=ALU.mult, op1=ALU.add,
                )

        result = keep.tile([P, ROW_TILES, HIDDEN], F32)

        def elu_and_store(i):
            grown = work.tile([P, HIDDEN], F32)
            if in_scalar_team(i):
                turned_sb = work.tile([P, BLOCKS, P], F32)
                nc.scalar.copy(out=turned_sb[:], in_=turned_sums[i][:])
                total_ps = psum_scalar.tile([P, HIDDEN], F32, tag="product")
                nc.tensor.matmul(out=total_ps[:], lhsT=coeff_t[:, i, :], rhs=bias_rows[:], start=True, stop=False)
                for b in range(BLOCKS):
                    nc.tensor.matmul(
                        out=total_ps[:, b * P : (b + 1) * P], lhsT=turned_sb[:, b, :], rhs=ident_f32[:], is_transpose=True,
                        start=False, stop=(b == BLOCKS - 1),
                    )
                nc.scalar.activation(out=grown[:], in_=total_ps[:], func=ACT.Exp)
                shrunk = work.tile([P, HIDDEN], F32)
                nc.scalar.activation(out=shrunk[:], in_=grown[:], func=ACT.Relu, scale=-1.0, bias=1.0)
                nc.vector.scalar_tensor_tensor(
                    out=result[:, i, :], in0=shrunk[:], scalar=-1.0, in1=total_ps[:], op0=ALU.mult, op1=ALU.max
                )
            else:
                nc.scalar.activation(out=grown[:], in_=acc[:, i, :], func=ACT.Exp)
                positive = work.tile([P, HIDDEN], F32)
                nc.vector.tensor_scalar(out=positive[:], in0=acc[:, i, :], scalar1=0.0, scalar2=None, op0=ALU.max)
                nc.vector.scalar_tensor_tensor(
                    out=result[:, i, :], in0=grown[:], scalar=-1.0, in1=positive[:], op0=ALU.add, op1=ALU.min
                )
            nc.sync.dma_start(out=out_rows[:, i, :], in_=result[:, i, :])

        regroup_expert(0)
        quantise_experts(0, 1)
        regroup_expert(1)
        quantise_experts(1, 1)
        for e in range(EXPERTS):
            if e + 2 < EXPERTS:
                regroup_expert(e + 2)
            for i in range(ROW_TILES):
                add_expert(e, i)
                if e == EXPERTS - 1:
                    elu_and_store(i)
                if i == ROW_TILES // 2 - 1 and e % 2 == 1 and e + 2 < EXPERTS:
                    quantise_experts(e + 1, 2)
